import numpy as np
import ml_dtypes

BF16 = ml_dtypes.bfloat16


def bf(x):
    return np.asarray(x, np.float32).astype(BF16)


def f32(x):
    return np.asarray(x, np.float32)


def f64(x):
    return np.asarray(x).astype(np.float64)


def striped(idx):
    return np.tile(idx.reshape(-1, 16).T, (8, 1))


C, F, S, N = 768, 3072, 256, 128
ERF_CUT, ERF_TERMS = 6.0, 150


def erf(a):
    c = np.clip(a, -ERF_CUT, ERF_CUT)
    term = c.copy()
    total = c.copy()
    for n in range(1, ERF_TERMS):
        term = term * (2.0 * c * c / (2 * n + 1))
        total = total + term
    return np.where(np.abs(a) > ERF_CUT, np.sign(a), 2.0 / np.sqrt(np.pi) * np.exp(-c * c) * total)


def gelu_erf(v):
    return 0.5 * v * (1.0 + erf(v / np.sqrt(2.0)))


def setup_inputs():
    return {"base": f32(np.random.standard_normal((C, S))), "x": bf(np.random.standard_normal((C, N))), "w1": bf(np.random.standard_normal((C, F)) / np.sqrt(C)), "b1": f32(0.1 * np.random.standard_normal((F, 1))), "w2": bf(np.random.standard_normal((F, C)) / np.sqrt(F)), "b2": f32(0.1 * np.random.standard_normal((C, 1))), "offs": striped(np.random.permutation(S)[:N])}


def reference(base, x, w1, b1, w2, b2, offs):
    idx = offs[:16].T.reshape(-1)
    h = gelu_erf(f64(w1).T @ f64(x) + f64(b1))
    ff = f64(w2).T @ h + f64(b2)
    out = f64(base).copy()
    out[:, idx] = f64(x) + ff
    return out

@@ -1,0 +1,101 @@
+import concourse.mybir as mybir
+from concourse.masks import make_identity
+
+P = 128
+C, F, S, N = 768, 3072, 256, 128
+CB = C // P
+FB = F // P
+CHUNK = 4
+NCHUNK = FB // CHUNK
+
+FLOPS = 2 * 2 * C * F * N
+
+BF16, F32, U16 = mybir.dt.bfloat16, mybir.dt.float32, mybir.dt.uint16
+GELU = mybir.ActivationFunctionType.Gelu
+IDENTITY = mybir.ActivationFunctionType.Identity
+ADD = mybir.AluOpType.add
+
+
+def tile_block_kernel(tc, base, x, w1, b1, w2, b2, offs, out):
+    nc = tc.nc
+    with (
+        tc.tile_pool(name="held", bufs=1) as held,
+        tc.tile_pool(name="work", bufs=3) as work,
+        tc.psum_pool(name="psum_h", bufs=2) as psum_h,
+        tc.psum_pool(name="psum_ff", bufs=1) as psum_ff,
+    ):
+        offsets = held.tile([P, N // 16], U16, name="offsets")
+        nc.sync.dma_start(offsets[:], offs)
+
+        x_bf = held.tile([P, CB, N], BF16, name="x_bf")
+        nc.sync.dma_start(x_bf[:], x.rearrange("(kb p) j -> p kb j", p=P))
+
+        bias_rows = held.tile([P, P], F32, name="bias_rows")
+        nc.vector.memset(bias_rows[:], 0.0)
+        nc.scalar.dma_start(bias_rows[0:FB, :], b1.rearrange("(fb p) o -> fb (p o)", p=P))
+        nc.scalar.dma_start(bias_rows[FB : FB + CB, :], b2.rearrange("(cb p) o -> cb (p o)", p=P))
+
+        w1_view = w1.rearrange("(kb p) f -> p kb f", p=P)
+        w1_sb = []
+        for ch in range(NCHUNK):
+            w1_chunk = held.tile([P, CB, CHUNK * P], BF16, name=f"w1_chunk{ch}")
+            nc.sync.dma_start(w1_chunk[:], w1_view[:, :, ch * CHUNK * P : (ch + 1) * CHUNK * P])
+            w1_sb.append(w1_chunk)
+
+        windows = []
+        for cb in range(CB):
+            window = held.tile([P, S], F32, name=f"window{cb}")
+            nc.sync.dma_start(window[:], base[cb * P : (cb + 1) * P, :])
+            windows.append(window)
+
+        w2_view = w2.rearrange("(fb p) c -> p fb c", p=P)
+        w2_sb = []
+        for ch in range(NCHUNK):
+            w2_chunk = held.tile([P, CHUNK, C], BF16, name=f"w2_chunk{ch}")
+            nc.sync.dma_start(w2_chunk[:], w2_view[:, ch * CHUNK : (ch + 1) * CHUNK, :])
+            w2_sb.append(w2_chunk)
+
+        identity = held.tile([P, P], F32, name="identity")
+        make_identity(nc, identity[:])
+        bias_ps = psum_h.tile([P, P], F32, name="bias_ps", tag="h_ps")
+        nc.tensor.transpose(bias_ps[:], bias_rows[:], identity[:])
+        bias_cols = held.tile([P, FB + CB], F32, name="bias_cols")
+        nc.vector.tensor_copy(bias_cols[:], bias_ps[:, 0 : FB + CB])
+
+        x_f32 = held.tile([P, CB, N], F32, name="x_f32")
+        nc.vector.tensor_copy(x_f32[:], x_bf[:])
+
+        h_sb = []
+        for fb in range(FB):
+            ch, i = divmod(fb, CHUNK)
+            h_ps = psum_h.tile([P, N], F32, name="h_ps", tag="h_ps")
+            for kb in range(CB):
+                nc.tensor.matmul(
+                    h_ps[:],
+                    w1_sb[ch][:, kb, i * P : (i + 1) * P],
+                    x_bf[:, kb, :],
+                    start=(kb == 0),
+                    stop=(kb == CB - 1),
+                )
+            h_block = held.tile([P, N], BF16, name=f"h_block{fb}")
+            nc.scalar.activation(h_block[:], h_ps[:], GELU, bias=bias_cols[:, fb : fb + 1])
+            h_sb.append(h_block)
+
+        ff_ps = [psum_ff.tile([P, N], F32, name=f"ff_ps{cb}") for cb in range(CB)]
+        for ch in range(NCHUNK):
+            for cb in range(CB):
+                for i in range(CHUNK):
+                    fb = ch * CHUNK + i
+                    nc.tensor.matmul(
+                        ff_ps[cb][:],
+                        w2_sb[ch][:, i, cb * P : (cb + 1) * P],
+                        h_sb[fb][:],
+                        start=(fb == 0),
+                        stop=(fb == FB - 1),
+                    )
+
+        for cb in range(CB):
+            ff = work.tile([P, N], F32, name="ff")
+            nc.scalar.activation(ff[:], ff_ps[cb][:], IDENTITY, bias=bias_cols[:, FB + cb : FB + cb + 1])
+            nc.vector.tensor_tensor(windows[cb][:].indirect(offsets[:]), ff[:], x_f32[:, cb, :], ADD)
+            nc.sync.dma_start(out[cb * P : (cb + 1) * P, :], windows[cb][:])

@@ -5,8 +5,12 @@ P = 128
 C, F, S, N = 768, 3072, 256, 128
 CB = C // P
 FB = F // P
-CHUNK = 4
-NCHUNK = FB // CHUNK
+NB = FB + CB
+W1_BLOCKS = 2
+W2_BLOCKS = 4
+GROUPS = ((0, 1), (2, 3), (4, 5))
+WARM_COLS = 512
+WARM_MATMULS = 7
 
 FLOPS = 2 * 2 * C * F * N
 
@@ -21,53 +25,63 @@ def tile_block_kernel(tc, base, x, w1, b1, w2, b2, offs, out):
     with (
         tc.tile_pool(name="held", bufs=1) as held,
         tc.tile_pool(name="work", bufs=3) as work,
-        tc.psum_pool(name="psum_h", bufs=2) as psum_h,
-        tc.psum_pool(name="psum_ff", bufs=1) as psum_ff,
+        tc.psum_pool(name="psum_h", bufs=4) as psum_h,
+        tc.psum_pool(name="psum_ff", bufs=4) as psum_ff,
     ):
-        offsets = held.tile([P, N // 16], U16, name="offsets")
-        nc.sync.dma_start(offsets[:], offs)
-
         x_bf = held.tile([P, CB, N], BF16, name="x_bf")
         nc.sync.dma_start(x_bf[:], x.rearrange("(kb p) j -> p kb j", p=P))
 
-        bias_rows = held.tile([P, P], F32, name="bias_rows")
-        nc.vector.memset(bias_rows[:], 0.0)
-        nc.scalar.dma_start(bias_rows[0:FB, :], b1.rearrange("(fb p) o -> fb (p o)", p=P))
-        nc.scalar.dma_start(bias_rows[FB : FB + CB, :], b2.rearrange("(cb p) o -> cb (p o)", p=P))
+        bias_rows = held.tile([NB, P], F32, name="bias_rows")
+        nc.sync.dma_start(bias_rows[0:FB, :], b1.rearrange("(fb p) o -> fb (p o)", p=P))
+        nc.sync.dma_start(bias_rows[FB:NB, :], b2.rearrange("(cb p) o -> cb (p o)", p=P))
+
+        offsets = held.tile([P, N // 16], U16, name="offsets")
+        nc.sync.dma_start(offsets[:], offs)
 
         w1_view = w1.rearrange("(kb p) f -> p kb f", p=P)
         w1_sb = []
-        for ch in range(NCHUNK):
-            w1_chunk = held.tile([P, CB, CHUNK * P], BF16, name=f"w1_chunk{ch}")
-            nc.sync.dma_start(w1_chunk[:], w1_view[:, :, ch * CHUNK * P : (ch + 1) * CHUNK * P])
+        for ch in range(FB // W1_BLOCKS):
+            w1_chunk = held.tile([P, CB, W1_BLOCKS * P], BF16, name=f"w1_chunk{ch}")
+            nc.sync.dma_start(w1_chunk[:], w1_view[:, :, ch * W1_BLOCKS * P : (ch + 1) * W1_BLOCKS * P])
             w1_sb.append(w1_chunk)
-
-        windows = []
-        for cb in range(CB):
-            window = held.tile([P, S], F32, name=f"window{cb}")
-            nc.sync.dma_start(window[:], base[cb * P : (cb + 1) * P, :])
-            windows.append(window)
 
         w2_view = w2.rearrange("(fb p) c -> p fb c", p=P)
         w2_sb = []
-        for ch in range(NCHUNK):
-            w2_chunk = held.tile([P, CHUNK, C], BF16, name=f"w2_chunk{ch}")
-            nc.sync.dma_start(w2_chunk[:], w2_view[:, ch * CHUNK : (ch + 1) * CHUNK, :])
-            w2_sb.append(w2_chunk)
+        windows = {}
+        for group in GROUPS:
+            pieces = []
+            for pc in range(FB // W2_BLOCKS):
+                w2_piece = held.tile([P, W2_BLOCKS, len(group) * P], BF16, name=f"w2_piece{group[0]}_{pc}")
+                nc.sync.dma_start(
+                    w2_piece[:],
+                    w2_view[:, pc * W2_BLOCKS : (pc + 1) * W2_BLOCKS, group[0] * P : (group[-1] + 1) * P],
+                )
+                pieces.append(w2_piece)
+            w2_sb.append(pieces)
+            for cb in group:
+                window = held.tile([P, S], F32, name=f"window{cb}")
+                nc.sync.dma_start(window[:], base[cb * P : (cb + 1) * P, :])
+                windows[cb] = window
 
-        identity = held.tile([P, P], F32, name="identity")
+        zeros = held.tile([P, WARM_COLS], BF16, name="zeros")
+        nc.vector.memset(zeros[:], 0.0)
+        warm_ps = psum_h.tile([P, WARM_COLS], F32, name="warm_ps", tag="h_ps")
+        for r in range(WARM_MATMULS):
+            nc.tensor.matmul(warm_ps[:], zeros[:, 0:P], zeros[:], start=True, stop=True)
+
+        identity = held.tile([NB, NB], F32, name="identity")
         make_identity(nc, identity[:])
-        bias_ps = psum_h.tile([P, P], F32, name="bias_ps", tag="h_ps")
-        nc.tensor.transpose(bias_ps[:], bias_rows[:], identity[:])
-        bias_cols = held.tile([P, FB + CB], F32, name="bias_cols")
-        nc.vector.tensor_copy(bias_cols[:], bias_ps[:, 0 : FB + CB])
+        bias_ps = psum_h.tile([P, NB], F32, name="bias_ps", tag="h_ps")
+        nc.tensor.matmul(bias_ps[:], bias_rows[:], identity[:], start=True, stop=True)
+        bias_cols = held.tile([P, NB], F32, name="bias_cols")
+        nc.vector.tensor_copy(bias_cols[:], bias_ps[:])
 
         x_f32 = held.tile([P, CB, N], F32, name="x_f32")
         nc.vector.tensor_copy(x_f32[:], x_bf[:])
 
         h_sb = []
         for fb in range(FB):
-            ch, i = divmod(fb, CHUNK)
+            ch, i = divmod(fb, W1_BLOCKS)
             h_ps = psum_h.tile([P, N], F32, name="h_ps", tag="h_ps")
             for kb in range(CB):
                 nc.tensor.matmul(
@@ -81,21 +95,22 @@ def tile_block_kernel(tc, base, x, w1, b1, w2, b2, offs, out):
             nc.scalar.activation(h_block[:], h_ps[:], GELU, bias=bias_cols[:, fb : fb + 1])
             h_sb.append(h_block)
 
-        ff_ps = [psum_ff.tile([P, N], F32, name=f"ff_ps{cb}") for cb in range(CB)]
-        for ch in range(NCHUNK):
-            for cb in range(CB):
-                for i in range(CHUNK):
-                    fb = ch * CHUNK + i
-                    nc.tensor.matmul(
-                        ff_ps[cb][:],
-                        w2_sb[ch][:, i, cb * P : (cb + 1) * P],
-                        h_sb[fb][:],
-                        start=(fb == 0),
-                        stop=(fb == FB - 1),
-                    )
-
-        for cb in range(CB):
-            ff = work.tile([P, N], F32, name="ff")
-            nc.scalar.activation(ff[:], ff_ps[cb][:], IDENTITY, bias=bias_cols[:, FB + cb : FB + cb + 1])
-            nc.vector.tensor_tensor(windows[cb][:].indirect(offsets[:]), ff[:], x_f32[:, cb, :], ADD)
-            nc.sync.dma_start(out[cb * P : (cb + 1) * P, :], windows[cb][:])
+        for group, pieces in zip(GROUPS, w2_sb):
+            ff_ps = [psum_ff.tile([P, N], F32, name=f"ff_ps{k}", tag="ff_ps") for k in range(len(group))]
+            for pc in range(FB // W2_BLOCKS):
+                for k in range(len(group)):
+                    for i in range(W2_BLOCKS):
+                        fb = pc * W2_BLOCKS + i
+                        nc.tensor.matmul(
+                            ff_ps[k][:],
+                            pieces[pc][:, i, k * P : (k + 1) * P],
+                            h_sb[fb][:],
+                            start=(fb == 0),
+                            stop=(fb == FB - 1),
+                        )
+            for k in range(len(group)):
+                cb = group[k]
+                ff = work.tile([P, N], F32, name="ff")
+                nc.scalar.activation(ff[:], ff_ps[k][:], IDENTITY, bias=bias_cols[:, FB + cb : FB + cb + 1])
+                nc.vector.tensor_tensor(windows[cb][:].indirect(offsets[:]), ff[:], x_f32[:, cb, :], ADD)
+                nc.sync.dma_start(out[cb * P : (cb + 1) * P, :], windows[cb][:])

@@ -6,10 +6,10 @@ C, F, S, N = 768, 3072, 256, 128
 CB = C // P
 FB = F // P
 NB = FB + CB
-W1_BLOCKS = 2
+BANK = 512
+H_IN_BANK = BANK // N
+FF_IN_BANK = 3
 W2_BLOCKS = 4
-GROUPS = ((0, 1), (2, 3), (4, 5))
-WARM_COLS = 512
 WARM_MATMULS = 7
 
 FLOPS = 2 * 2 * C * F * N
@@ -25,8 +25,7 @@ def tile_block_kernel(tc, base, x, w1, b1, w2, b2, offs, out):
     with (
         tc.tile_pool(name="held", bufs=1) as held,
         tc.tile_pool(name="work", bufs=3) as work,
-        tc.psum_pool(name="psum_h", bufs=4) as psum_h,
-        tc.psum_pool(name="psum_ff", bufs=4) as psum_ff,
+        tc.psum_pool(name="psum", bufs=8) as psum,
     ):
         x_bf = held.tile([P, CB, N], BF16, name="x_bf")
         nc.sync.dma_start(x_bf[:], x.rearrange("(kb p) j -> p kb j", p=P))
@@ -38,40 +37,34 @@ def tile_block_kernel(tc, base, x, w1, b1, w2, b2, offs, out):
         offsets = held.tile([P, N // 16], U16, name="offsets")
         nc.sync.dma_start(offsets[:], offs)
 
-        w1_view = w1.rearrange("(kb p) f -> p kb f", p=P)
         w1_sb = []
-        for ch in range(FB // W1_BLOCKS):
-            w1_chunk = held.tile([P, CB, W1_BLOCKS * P], BF16, name=f"w1_chunk{ch}")
-            nc.sync.dma_start(w1_chunk[:], w1_view[:, :, ch * W1_BLOCKS * P : (ch + 1) * W1_BLOCKS * P])
-            w1_sb.append(w1_chunk)
+        for kb in range(CB):
+            w1_rows = held.tile([P, F], BF16, name=f"w1_rows{kb}")
+            nc.sync.dma_start(w1_rows[:], w1[kb * P : (kb + 1) * P, :])
+            w1_sb.append(w1_rows)
 
         w2_view = w2.rearrange("(fb p) c -> p fb c", p=P)
         w2_sb = []
-        windows = {}
-        for group in GROUPS:
-            pieces = []
-            for pc in range(FB // W2_BLOCKS):
-                w2_piece = held.tile([P, W2_BLOCKS, len(group) * P], BF16, name=f"w2_piece{group[0]}_{pc}")
-                nc.sync.dma_start(
-                    w2_piece[:],
-                    w2_view[:, pc * W2_BLOCKS : (pc + 1) * W2_BLOCKS, group[0] * P : (group[-1] + 1) * P],
-                )
-                pieces.append(w2_piece)
-            w2_sb.append(pieces)
-            for cb in group:
-                window = held.tile([P, S], F32, name=f"window{cb}")
-                nc.sync.dma_start(window[:], base[cb * P : (cb + 1) * P, :])
-                windows[cb] = window
+        for ch in range(FB // W2_BLOCKS):
+            w2_rows = held.tile([P, W2_BLOCKS, C], BF16, name=f"w2_rows{ch}")
+            nc.sync.dma_start(w2_rows[:], w2_view[:, ch * W2_BLOCKS : (ch + 1) * W2_BLOCKS, :])
+            w2_sb.append(w2_rows)
 
-        zeros = held.tile([P, WARM_COLS], BF16, name="zeros")
+        windows = []
+        for cb in range(CB):
+            window = held.tile([P, S], F32, name=f"window{cb}")
+            nc.sync.dma_start(window[:], base[cb * P : (cb + 1) * P, :])
+            windows.append(window)
+
+        zeros = held.tile([P, BANK], BF16, name="zeros")
         nc.vector.memset(zeros[:], 0.0)
-        warm_ps = psum_h.tile([P, WARM_COLS], F32, name="warm_ps", tag="h_ps")
+        warm_ps = psum.tile([P, BANK], F32, name="warm_ps", tag="bank")
         for r in range(WARM_MATMULS):
             nc.tensor.matmul(warm_ps[:], zeros[:, 0:P], zeros[:], start=True, stop=True)
 
         identity = held.tile([NB, NB], F32, name="identity")
         make_identity(nc, identity[:])
-        bias_ps = psum_h.tile([P, NB], F32, name="bias_ps", tag="h_ps")
+        bias_ps = psum.tile([P, NB], F32, name="bias_ps", tag="bank")
         nc.tensor.matmul(bias_ps[:], bias_rows[:], identity[:], start=True, stop=True)
         bias_cols = held.tile([P, NB], F32, name="bias_cols")
         nc.vector.tensor_copy(bias_cols[:], bias_ps[:])
@@ -79,38 +72,43 @@ def tile_block_kernel(tc, base, x, w1, b1, w2, b2, offs, out):
         x_f32 = held.tile([P, CB, N], F32, name="x_f32")
         nc.vector.tensor_copy(x_f32[:], x_bf[:])
 
+        h_ps = [psum.tile([P, BANK], F32, name=f"h_ps{b}", tag="bank") for b in range(FB // H_IN_BANK)]
+        for kb in range(CB):
+            for fb in range(FB):
+                b, i = divmod(fb, H_IN_BANK)
+                nc.tensor.matmul(
+                    h_ps[b][:, i * N : (i + 1) * N],
+                    w1_sb[kb][:, fb * P : (fb + 1) * P],
+                    x_bf[:, kb, :],
+                    start=(kb == 0 and i == 0),
+                    stop=(kb == CB - 1 and i == H_IN_BANK - 1),
+                )
+
         h_sb = []
         for fb in range(FB):
-            ch, i = divmod(fb, W1_BLOCKS)
-            h_ps = psum_h.tile([P, N], F32, name="h_ps", tag="h_ps")
-            for kb in range(CB):
-                nc.tensor.matmul(
-                    h_ps[:],
-                    w1_sb[ch][:, kb, i * P : (i + 1) * P],
-                    x_bf[:, kb, :],
-                    start=(kb == 0),
-                    stop=(kb == CB - 1),
-                )
+            b, i = divmod(fb, H_IN_BANK)
             h_block = held.tile([P, N], BF16, name=f"h_block{fb}")
-            nc.scalar.activation(h_block[:], h_ps[:], GELU, bias=bias_cols[:, fb : fb + 1])
+            nc.scalar.activation(h_block[:], h_ps[b][:, i * N : (i + 1) * N], GELU, bias=bias_cols[:, fb : fb + 1])
             h_sb.append(h_block)
 
-        for group, pieces in zip(GROUPS, w2_sb):
-            ff_ps = [psum_ff.tile([P, N], F32, name=f"ff_ps{k}", tag="ff_ps") for k in range(len(group))]
-            for pc in range(FB // W2_BLOCKS):
-                for k in range(len(group)):
-                    for i in range(W2_BLOCKS):
-                        fb = pc * W2_BLOCKS + i
-                        nc.tensor.matmul(
-                            ff_ps[k][:],
-                            pieces[pc][:, i, k * P : (k + 1) * P],
-                            h_sb[fb][:],
-                            start=(fb == 0),
-                            stop=(fb == FB - 1),
-                        )
-            for k in range(len(group)):
-                cb = group[k]
-                ff = work.tile([P, N], F32, name="ff")
-                nc.scalar.activation(ff[:], ff_ps[k][:], IDENTITY, bias=bias_cols[:, FB + cb : FB + cb + 1])
-                nc.vector.tensor_tensor(windows[cb][:].indirect(offsets[:]), ff[:], x_f32[:, cb, :], ADD)
-                nc.sync.dma_start(out[cb * P : (cb + 1) * P, :], windows[cb][:])
+        ff_ps = [psum.tile([P, FF_IN_BANK * N], F32, name=f"ff_ps{b}", tag="bank") for b in range(CB // FF_IN_BANK)]
+        for fb in range(FB):
+            ch, r = divmod(fb, W2_BLOCKS)
+            for cb in range(CB):
+                b, i = divmod(cb, FF_IN_BANK)
+                nc.tensor.matmul(
+                    ff_ps[b][:, i * N : (i + 1) * N],
+                    w2_sb[ch][:, r, cb * P : (cb + 1) * P],
+                    h_sb[fb][:],
+                    start=(fb == 0 and i == 0),
+                    stop=(fb == FB - 1 and i == FF_IN_BANK - 1),
+                )
+
+        for cb in range(CB):
+            b, i = divmod(cb, FF_IN_BANK)
+            ff = work.tile([P, N], F32, name="ff")
+            nc.scalar.activation(
+                ff[:], ff_ps[b][:, i * N : (i + 1) * N], IDENTITY, bias=bias_cols[:, FB + cb : FB + cb + 1]
+            )
+            nc.vector.tensor_tensor(windows[cb][:].indirect(offsets[:]), ff[:], x_f32[:, cb, :], ADD)
+            nc.sync.dma_start(out[cb * P : (cb + 1) * P, :], windows[cb][:])

@@ -8,7 +8,8 @@ FB = F // P
 NB = FB + CB
 BANK = 512
 H_IN_BANK = BANK // N
-FF_IN_BANK = 3
+PARTS = 2
+PART_FB = FB // PARTS
 W2_BLOCKS = 4
 WARM_MATMULS = 7
 
@@ -38,10 +39,15 @@ def tile_block_kernel(tc, base, x, w1, b1, w2, b2, offs, out):
         nc.sync.dma_start(offsets[:], offs)
 
         w1_sb = []
-        for kb in range(CB):
-            w1_rows = held.tile([P, F], BF16, name=f"w1_rows{kb}")
-            nc.sync.dma_start(w1_rows[:], w1[kb * P : (kb + 1) * P, :])
-            w1_sb.append(w1_rows)
+        for part in range(PARTS):
+            w1_part = []
+            for kb in range(CB):
+                w1_rows = held.tile([P, PART_FB * P], BF16, name=f"w1_rows{part}_{kb}")
+                nc.sync.dma_start(
+                    w1_rows[:], w1[kb * P : (kb + 1) * P, part * PART_FB * P : (part + 1) * PART_FB * P]
+                )
+                w1_part.append(w1_rows)
+            w1_sb.append(w1_part)
 
         w2_view = w2.rearrange("(fb p) c -> p fb c", p=P)
         w2_sb = []
@@ -72,43 +78,41 @@ def tile_block_kernel(tc, base, x, w1, b1, w2, b2, offs, out):
         x_f32 = held.tile([P, CB, N], F32, name="x_f32")
         nc.vector.tensor_copy(x_f32[:], x_bf[:])
 
-        h_ps = [psum.tile([P, BANK], F32, name=f"h_ps{b}", tag="bank") for b in range(FB // H_IN_BANK)]
-        for kb in range(CB):
-            for fb in range(FB):
-                b, i = divmod(fb, H_IN_BANK)
-                nc.tensor.matmul(
-                    h_ps[b][:, i * N : (i + 1) * N],
-                    w1_sb[kb][:, fb * P : (fb + 1) * P],
-                    x_bf[:, kb, :],
-                    start=(kb == 0 and i == 0),
-                    stop=(kb == CB - 1 and i == H_IN_BANK - 1),
-                )
-
         h_sb = []
-        for fb in range(FB):
-            b, i = divmod(fb, H_IN_BANK)
-            h_block = held.tile([P, N], BF16, name=f"h_block{fb}")
-            nc.scalar.activation(h_block[:], h_ps[b][:, i * N : (i + 1) * N], GELU, bias=bias_cols[:, fb : fb + 1])
-            h_sb.append(h_block)
+        for part in range(PARTS):
+            h_ps = [psum.tile([P, BANK], F32, name=f"h_ps{b}", tag="bank") for b in range(PART_FB // H_IN_BANK)]
+            for kb in range(CB):
+                for t in range(PART_FB):
+                    b, i = divmod(t, H_IN_BANK)
+                    nc.tensor.matmul(
+                        h_ps[b][:, i * N : (i + 1) * N],
+                        w1_sb[part][kb][:, t * P : (t + 1) * P],
+                        x_bf[:, kb, :],
+                        start=(kb == 0 and i == 0),
+                        stop=(kb == CB - 1 and i == H_IN_BANK - 1),
+                    )
+            for t in range(PART_FB):
+                b, i = divmod(t, H_IN_BANK)
+                fb = part * PART_FB + t
+                h_block = held.tile([P, N], BF16, name=f"h_block{fb}")
+                nc.scalar.activation(h_block[:], h_ps[b][:, i * N : (i + 1) * N], GELU, bias=bias_cols[:, fb : fb + 1])
+                h_sb.append(h_block)
 
-        ff_ps = [psum.tile([P, FF_IN_BANK * N], F32, name=f"ff_ps{b}", tag="bank") for b in range(CB // FF_IN_BANK)]
-        for fb in range(FB):
-            ch, r = divmod(fb, W2_BLOCKS)
+        ff_ps = [psum.tile([P, N], F32, name=f"ff_ps{cb}", tag="bank") for cb in range(CB)]
+        for ch in range(FB // W2_BLOCKS):
             for cb in range(CB):
-                b, i = divmod(cb, FF_IN_BANK)
-                nc.tensor.matmul(
-                    ff_ps[b][:, i * N : (i + 1) * N],
-                    w2_sb[ch][:, r, cb * P : (cb + 1) * P],
-                    h_sb[fb][:],
-                    start=(fb == 0 and i == 0),
-                    stop=(fb == FB - 1 and i == FF_IN_BANK - 1),
-                )
+                for r in range(W2_BLOCKS):
+                    fb = ch * W2_BLOCKS + r
+                    nc.tensor.matmul(
+                        ff_ps[cb][:],
+                        w2_sb[ch][:, r, cb * P : (cb + 1) * P],
+                        h_sb[fb][:],
+                        start=(fb == 0),
+                        stop=(fb == FB - 1),
+                    )
 
         for cb in range(CB):
-            b, i = divmod(cb, FF_IN_BANK)
             ff = work.tile([P, N], F32, name="ff")
-            nc.scalar.activation(
-                ff[:], ff_ps[b][:, i * N : (i + 1) * N], IDENTITY, bias=bias_cols[:, FB + cb : FB + cb + 1]
-            )
+            nc.scalar.activation(ff[:], ff_ps[cb][:], IDENTITY, bias=bias_cols[:, FB + cb : FB + cb + 1])
             nc.vector.tensor_tensor(windows[cb][:].indirect(offsets[:]), ff[:], x_f32[:, cb, :], ADD)
             nc.sync.dma_start(out[cb * P : (cb + 1) * P, :], windows[cb][:])

@@ -5,12 +5,12 @@ P = 128
 C, F, S, N = 768, 3072, 256, 128
 CB = C // P
 FB = F // P
-NB = FB + CB
 BANK = 512
 H_IN_BANK = BANK // N
 PARTS = 2
 PART_FB = FB // PARTS
-W2_BLOCKS = 4
+R = 4
+CHUNKS = FB // R
 WARM_MATMULS = 7
 
 FLOPS = 2 * 2 * C * F * N
@@ -31,9 +31,10 @@ def tile_block_kernel(tc, base, x, w1, b1, w2, b2, offs, out):
         x_bf = held.tile([P, CB, N], BF16, name="x_bf")
         nc.sync.dma_start(x_bf[:], x.rearrange("(kb p) j -> p kb j", p=P))
 
-        bias_rows = held.tile([NB, P], F32, name="bias_rows")
-        nc.sync.dma_start(bias_rows[0:FB, :], b1.rearrange("(fb p) o -> fb (p o)", p=P))
-        nc.sync.dma_start(bias_rows[FB:NB, :], b2.rearrange("(cb p) o -> cb (p o)", p=P))
+        assert CHUNKS == CB
+        bias_rows = held.tile([CB, (R + 1) * P], F32, name="bias_rows")
+        nc.sync.dma_start(bias_rows[:, 0 : R * P], b1.rearrange("(ch m) o -> ch (m o)", ch=CHUNKS))
+        nc.sync.dma_start(bias_rows[:, R * P : (R + 1) * P], b2.rearrange("(cb p) o -> cb (p o)", p=P))
 
         offsets = held.tile([P, N // 16], U16, name="offsets")
         nc.sync.dma_start(offsets[:], offs)
@@ -49,11 +50,11 @@ def tile_block_kernel(tc, base, x, w1, b1, w2, b2, offs, out):
                 w1_part.append(w1_rows)
             w1_sb.append(w1_part)
 
-        w2_view = w2.rearrange("(fb p) c -> p fb c", p=P)
+        w2_view = w2.rearrange("(ch p r) c -> ch p r c", p=P, r=R)
         w2_sb = []
-        for ch in range(FB // W2_BLOCKS):
-            w2_rows = held.tile([P, W2_BLOCKS, C], BF16, name=f"w2_rows{ch}")
-            nc.sync.dma_start(w2_rows[:], w2_view[:, ch * W2_BLOCKS : (ch + 1) * W2_BLOCKS, :])
+        for ch in range(CHUNKS):
+            w2_rows = held.tile([P, R, C], BF16, name=f"w2_rows{ch}")
+            nc.sync.dma_start(w2_rows[:], w2_view[ch])
             w2_sb.append(w2_rows)
 
         windows = []
@@ -68,11 +69,14 @@ def tile_block_kernel(tc, base, x, w1, b1, w2, b2, offs, out):
         for r in range(WARM_MATMULS):
             nc.tensor.matmul(warm_ps[:], zeros[:, 0:P], zeros[:], start=True, stop=True)
 
-        identity = held.tile([NB, NB], F32, name="identity")
+        identity = held.tile([CB, CB], F32, name="identity")
         make_identity(nc, identity[:])
-        bias_ps = psum.tile([P, NB], F32, name="bias_ps", tag="bank")
-        nc.tensor.matmul(bias_ps[:], bias_rows[:], identity[:], start=True, stop=True)
-        bias_cols = held.tile([P, NB], F32, name="bias_cols")
+        b1_rows = bias_rows[:, 0 : R * P].rearrange("ch (p r) -> ch r p", r=R)
+        bias_ps = psum.tile([P, R + 1, CB], F32, name="bias_ps", tag="bank")
+        for r in range(R):
+            nc.tensor.matmul(bias_ps[:, r, :], b1_rows[:, r, :], identity[:], start=True, stop=True)
+        nc.tensor.matmul(bias_ps[:, R, :], bias_rows[:, R * P : (R + 1) * P], identity[:], start=True, stop=True)
+        bias_cols = held.tile([P, R + 1, CB], F32, name="bias_cols")
         nc.vector.tensor_copy(bias_cols[:], bias_ps[:])
 
         x_f32 = held.tile([P, CB, N], F32, name="x_f32")
@@ -82,11 +86,12 @@ def tile_block_kernel(tc, base, x, w1, b1, w2, b2, offs, out):
         for part in range(PARTS):
             h_ps = [psum.tile([P, BANK], F32, name=f"h_ps{b}", tag="bank") for b in range(PART_FB // H_IN_BANK)]
             for kb in range(CB):
+                w1_blocks = w1_sb[part][kb][:].rearrange("k (ch p r) -> k ch r p", p=P, r=R)
                 for t in range(PART_FB):
                     b, i = divmod(t, H_IN_BANK)
                     nc.tensor.matmul(
                         h_ps[b][:, i * N : (i + 1) * N],
-                        w1_sb[part][kb][:, t * P : (t + 1) * P],
+                        w1_blocks[:, t // R, t % R, :],
                         x_bf[:, kb, :],
                         start=(kb == 0 and i == 0),
                         stop=(kb == CB - 1 and i == H_IN_BANK - 1),
@@ -95,14 +100,16 @@ def tile_block_kernel(tc, base, x, w1, b1, w2, b2, offs, out):
                 b, i = divmod(t, H_IN_BANK)
                 fb = part * PART_FB + t
                 h_block = held.tile([P, N], BF16, name=f"h_block{fb}")
-                nc.scalar.activation(h_block[:], h_ps[b][:, i * N : (i + 1) * N], GELU, bias=bias_cols[:, fb : fb + 1])
+                nc.scalar.activation(
+                    h_block[:], h_ps[b][:, i * N : (i + 1) * N], GELU, bias=bias_cols[:, fb % R, fb // R : fb // R + 1]
+                )
                 h_sb.append(h_block)
 
         ff_ps = [psum.tile([P, N], F32, name=f"ff_ps{cb}", tag="bank") for cb in range(CB)]
-        for ch in range(FB // W2_BLOCKS):
+        for ch in range(CHUNKS):
             for cb in range(CB):
-                for r in range(W2_BLOCKS):
-                    fb = ch * W2_BLOCKS + r
+                for r in range(R):
+                    fb = ch * R + r
                     nc.tensor.matmul(
                         ff_ps[cb][:],
                         w2_sb[ch][:, r, cb * P : (cb + 1) * P],
@@ -113,6 +120,6 @@ def tile_block_kernel(tc, base, x, w1, b1, w2, b2, offs, out):
 
         for cb in range(CB):
             ff = work.tile([P, N], F32, name="ff")
-            nc.scalar.activation(ff[:], ff_ps[cb][:], IDENTITY, bias=bias_cols[:, FB + cb : FB + cb + 1])
+            nc.scalar.activation(ff[:], ff_ps[cb][:], IDENTITY, bias=bias_cols[:, R, cb : cb + 1])
             nc.vector.tensor_tensor(windows[cb][:].indirect(offsets[:]), ff[:], x_f32[:, cb, :], ADD)
             nc.sync.dma_start(out[cb * P : (cb + 1) * P, :], windows[cb][:])

@@ -5,12 +5,12 @@ P = 128
 C, F, S, N = 768, 3072, 256, 128
 CB = C // P
 FB = F // P
-BANK = 512
-H_IN_BANK = BANK // N
-PARTS = 2
-PART_FB = FB // PARTS
 R = 4
 CHUNKS = FB // R
+PARTS = 2
+PART_FB = FB // PARTS
+BANK = 512
+H_IN_BANK = BANK // N
 WARM_MATMULS = 7
 
 FLOPS = 2 * 2 * C * F * N
@@ -28,25 +28,20 @@ def tile_block_kernel(tc, base, x, w1, b1, w2, b2, offs, out):
         tc.tile_pool(name="work", bufs=3) as work,
         tc.psum_pool(name="psum", bufs=8) as psum,
     ):
+
         x_bf = held.tile([P, CB, N], BF16, name="x_bf")
-        nc.sync.dma_start(x_bf[:], x.rearrange("(kb p) j -> p kb j", p=P))
+        nc.sync.dma_start(x_bf[:], x.rearrange("(p kb) j -> p kb j", kb=CB))
 
-        assert CHUNKS == CB
-        bias_rows = held.tile([CB, (R + 1) * P], F32, name="bias_rows")
-        nc.sync.dma_start(bias_rows[:, 0 : R * P], b1.rearrange("(ch m) o -> ch (m o)", ch=CHUNKS))
-        nc.sync.dma_start(bias_rows[:, R * P : (R + 1) * P], b2.rearrange("(cb p) o -> cb (p o)", p=P))
+        b1_rows = held.tile([CHUNKS, R * P], F32, name="b1_rows")
+        nc.sync.dma_start(b1_rows[:], b1.rearrange("(ch m) o -> ch (m o)", ch=CHUNKS))
 
-        offsets = held.tile([P, N // 16], U16, name="offsets")
-        nc.sync.dma_start(offsets[:], offs)
-
+        w1_view = w1.rearrange("(p kb) f -> kb p f", kb=CB)
         w1_sb = []
         for part in range(PARTS):
             w1_part = []
             for kb in range(CB):
                 w1_rows = held.tile([P, PART_FB * P], BF16, name=f"w1_rows{part}_{kb}")
-                nc.sync.dma_start(
-                    w1_rows[:], w1[kb * P : (kb + 1) * P, part * PART_FB * P : (part + 1) * PART_FB * P]
-                )
+                nc.sync.dma_start(w1_rows[:], w1_view[kb][:, part * PART_FB * P : (part + 1) * PART_FB * P])
                 w1_part.append(w1_rows)
             w1_sb.append(w1_part)
 
@@ -57,27 +52,32 @@ def tile_block_kernel(tc, base, x, w1, b1, w2, b2, offs, out):
             nc.sync.dma_start(w2_rows[:], w2_view[ch])
             w2_sb.append(w2_rows)
 
+        b2_cols = held.tile([P, CB], F32, name="b2_cols")
+        nc.sync.dma_start(b2_cols[:], b2.rearrange("(p cb) o -> p (cb o)", cb=CB))
+        offsets = held.tile([P, N // 16], U16, name="offsets")
+        nc.sync.dma_start(offsets[:], offs)
+        base_view = base.rearrange("(p cb) s -> cb p s", cb=CB)
+        out_view = out.rearrange("(p cb) s -> cb p s", cb=CB)
         windows = []
         for cb in range(CB):
             window = held.tile([P, S], F32, name=f"window{cb}")
-            nc.sync.dma_start(window[:], base[cb * P : (cb + 1) * P, :])
+            nc.sync.dma_start(window[:], base_view[cb])
             windows.append(window)
 
         zeros = held.tile([P, BANK], BF16, name="zeros")
         nc.vector.memset(zeros[:], 0.0)
         warm_ps = psum.tile([P, BANK], F32, name="warm_ps", tag="bank")
-        for r in range(WARM_MATMULS):
+        for w in range(WARM_MATMULS):
             nc.tensor.matmul(warm_ps[:], zeros[:, 0:P], zeros[:], start=True, stop=True)
 
-        identity = held.tile([CB, CB], F32, name="identity")
+        identity = held.tile([CHUNKS, CHUNKS], F32, name="identity")
         make_identity(nc, identity[:])
-        b1_rows = bias_rows[:, 0 : R * P].rearrange("ch (p r) -> ch r p", r=R)
-        bias_ps = psum.tile([P, R + 1, CB], F32, name="bias_ps", tag="bank")
+        b1_blocks = b1_rows[:].rearrange("ch (p r) -> ch r p", r=R)
+        b1_ps = psum.tile([P, R, CHUNKS], F32, name="b1_ps", tag="bank")
         for r in range(R):
-            nc.tensor.matmul(bias_ps[:, r, :], b1_rows[:, r, :], identity[:], start=True, stop=True)
-        nc.tensor.matmul(bias_ps[:, R, :], bias_rows[:, R * P : (R + 1) * P], identity[:], start=True, stop=True)
-        bias_cols = held.tile([P, R + 1, CB], F32, name="bias_cols")
-        nc.vector.tensor_copy(bias_cols[:], bias_ps[:])
+            nc.tensor.matmul(b1_ps[:, r, :], b1_blocks[:, r, :], identity[:], start=True, stop=True)
+        b1_cols = held.tile([P, R, CHUNKS], F32, name="b1_cols")
+        nc.vector.tensor_copy(b1_cols[:], b1_ps[:])
 
         x_f32 = held.tile([P, CB, N], F32, name="x_f32")
         nc.vector.tensor_copy(x_f32[:], x_bf[:])
@@ -98,28 +98,28 @@ def tile_block_kernel(tc, base, x, w1, b1, w2, b2, offs, out):
                     )
             for t in range(PART_FB):
                 b, i = divmod(t, H_IN_BANK)
-                fb = part * PART_FB + t
-                h_block = held.tile([P, N], BF16, name=f"h_block{fb}")
+                ch, r = divmod(part * PART_FB + t, R)
+                h_block = held.tile([P, N], BF16, name=f"h_block{ch}_{r}")
                 nc.scalar.activation(
-                    h_block[:], h_ps[b][:, i * N : (i + 1) * N], GELU, bias=bias_cols[:, fb % R, fb // R : fb // R + 1]
+                    h_block[:], h_ps[b][:, i * N : (i + 1) * N], GELU, bias=b1_cols[:, r, ch : ch + 1]
                 )
                 h_sb.append(h_block)
 
         ff_ps = [psum.tile([P, N], F32, name=f"ff_ps{cb}", tag="bank") for cb in range(CB)]
         for ch in range(CHUNKS):
+            w2_blocks = w2_sb[ch][:].rearrange("f r (p cb) -> f r cb p", cb=CB)
             for cb in range(CB):
                 for r in range(R):
-                    fb = ch * R + r
                     nc.tensor.matmul(
                         ff_ps[cb][:],
-                        w2_sb[ch][:, r, cb * P : (cb + 1) * P],
-                        h_sb[fb][:],
-                        start=(fb == 0),
-                        stop=(fb == FB - 1),
+                        w2_blocks[:, r, cb, :],
+                        h_sb[ch * R + r][:],
+                        start=(ch == 0 and r == 0),
+                        stop=(ch == CHUNKS - 1 and r == R - 1),
                     )
 
         for cb in range(CB):
             ff = work.tile([P, N], F32, name="ff")
-            nc.scalar.activation(ff[:], ff_ps[cb][:], IDENTITY, bias=bias_cols[:, R, cb : cb + 1])
+            nc.scalar.activation(ff[:], ff_ps[cb][:], IDENTITY, bias=b2_cols[:, cb : cb + 1])
             nc.vector.tensor_tensor(windows[cb][:].indirect(offsets[:]), ff[:], x_f32[:, cb, :], ADD)
-            nc.sync.dma_start(out[cb * P : (cb + 1) * P, :], windows[cb][:])
+            nc.sync.dma_start(out_view[cb], windows[cb][:])

@@ -11,7 +11,6 @@ PARTS = 2
 PART_FB = FB // PARTS
 BANK = 512
 H_IN_BANK = BANK // N
-WARM_MATMULS = 7
 
 FLOPS = 2 * 2 * C * F * N
 
@@ -63,12 +62,6 @@ def tile_block_kernel(tc, base, x, w1, b1, w2, b2, offs, out):
             window = held.tile([P, S], F32, name=f"window{cb}")
             nc.sync.dma_start(window[:], base_view[cb])
             windows.append(window)
-
-        zeros = held.tile([P, BANK], BF16, name="zeros")
-        nc.vector.memset(zeros[:], 0.0)
-        warm_ps = psum.tile([P, BANK], F32, name="warm_ps", tag="bank")
-        for w in range(WARM_MATMULS):
-            nc.tensor.matmul(warm_ps[:], zeros[:, 0:P], zeros[:], start=True, stop=True)
 
         identity = held.tile([CHUNKS, CHUNKS], F32, name="identity")
         make_identity(nc, identity[:])

@@ -9,6 +9,7 @@ R = 4
 CHUNKS = FB // R
 PARTS = 2
 PART_FB = FB // PARTS
+KB_IN_LOAD = 2
 BANK = 512
 H_IN_BANK = BANK // N
 
@@ -34,13 +35,15 @@ def tile_block_kernel(tc, base, x, w1, b1, w2, b2, offs, out):
         b1_rows = held.tile([CHUNKS, R * P], F32, name="b1_rows")
         nc.sync.dma_start(b1_rows[:], b1.rearrange("(ch m) o -> ch (m o)", ch=CHUNKS))
 
-        w1_view = w1.rearrange("(p kb) f -> kb p f", kb=CB)
+        w1_view = w1.rearrange("(p kb) f -> p kb f", kb=CB)
         w1_sb = []
         for part in range(PARTS):
             w1_part = []
-            for kb in range(CB):
-                w1_rows = held.tile([P, PART_FB * P], BF16, name=f"w1_rows{part}_{kb}")
-                nc.sync.dma_start(w1_rows[:], w1_view[kb][:, part * PART_FB * P : (part + 1) * PART_FB * P])
+            for kb in range(0, CB, KB_IN_LOAD):
+                w1_rows = held.tile([P, KB_IN_LOAD, PART_FB * P], BF16, name=f"w1_rows{part}_{kb}")
+                nc.sync.dma_start(
+                    w1_rows[:], w1_view[:, kb : kb + KB_IN_LOAD, part * PART_FB * P : (part + 1) * PART_FB * P]
+                )
                 w1_part.append(w1_rows)
             w1_sb.append(w1_part)
 
@@ -79,7 +82,7 @@ def tile_block_kernel(tc, base, x, w1, b1, w2, b2, offs, out):
         for part in range(PARTS):
             h_ps = [psum.tile([P, BANK], F32, name=f"h_ps{b}", tag="bank") for b in range(PART_FB // H_IN_BANK)]
             for kb in range(CB):
-                w1_blocks = w1_sb[part][kb][:].rearrange("k (ch p r) -> k ch r p", p=P, r=R)
+                w1_blocks = w1_sb[part][kb // KB_IN_LOAD][:, kb % KB_IN_LOAD, :].rearrange("k (ch p r) -> k ch r p", p=P, r=R)
                 for t in range(PART_FB):
                     b, i = divmod(t, H_IN_BANK)
                     nc.tensor.matmul(

@@ -9,7 +9,7 @@ R = 4
 CHUNKS = FB // R
 PARTS = 2
 PART_FB = FB // PARTS
-KB_IN_LOAD = 2
+KB_IN_LOAD = (1, 2)
 BANK = 512
 H_IN_BANK = BANK // N
 
@@ -33,16 +33,16 @@ def tile_block_kernel(tc, base, x, w1, b1, w2, b2, offs, out):
         nc.sync.dma_start(x_bf[:], x.rearrange("(p kb) j -> p kb j", kb=CB))
 
         b1_rows = held.tile([CHUNKS, R * P], F32, name="b1_rows")
-        nc.sync.dma_start(b1_rows[:], b1.rearrange("(ch m) o -> ch (m o)", ch=CHUNKS))
+        nc.scalar.dma_start(b1_rows[:], b1.rearrange("(ch m) o -> ch (m o)", ch=CHUNKS))
 
         w1_view = w1.rearrange("(p kb) f -> p kb f", kb=CB)
         w1_sb = []
         for part in range(PARTS):
             w1_part = []
-            for kb in range(0, CB, KB_IN_LOAD):
-                w1_rows = held.tile([P, KB_IN_LOAD, PART_FB * P], BF16, name=f"w1_rows{part}_{kb}")
+            for kb in range(0, CB, KB_IN_LOAD[part]):
+                w1_rows = held.tile([P, KB_IN_LOAD[part], PART_FB * P], BF16, name=f"w1_rows{part}_{kb}")
                 nc.sync.dma_start(
-                    w1_rows[:], w1_view[:, kb : kb + KB_IN_LOAD, part * PART_FB * P : (part + 1) * PART_FB * P]
+                    w1_rows[:], w1_view[:, kb : kb + KB_IN_LOAD[part], part * PART_FB * P : (part + 1) * PART_FB * P]
                 )
                 w1_part.append(w1_rows)
             w1_sb.append(w1_part)
@@ -66,23 +66,14 @@ def tile_block_kernel(tc, base, x, w1, b1, w2, b2, offs, out):
             nc.sync.dma_start(window[:], base_view[cb])
             windows.append(window)
 
-        identity = held.tile([CHUNKS, CHUNKS], F32, name="identity")
-        make_identity(nc, identity[:])
-        b1_blocks = b1_rows[:].rearrange("ch (p r) -> ch r p", r=R)
-        b1_ps = psum.tile([P, R, CHUNKS], F32, name="b1_ps", tag="bank")
-        for r in range(R):
-            nc.tensor.matmul(b1_ps[:, r, :], b1_blocks[:, r, :], identity[:], start=True, stop=True)
-        b1_cols = held.tile([P, R, CHUNKS], F32, name="b1_cols")
-        nc.vector.tensor_copy(b1_cols[:], b1_ps[:])
-
         x_f32 = held.tile([P, CB, N], F32, name="x_f32")
         nc.vector.tensor_copy(x_f32[:], x_bf[:])
 
-        h_sb = []
-        for part in range(PARTS):
+        def hidden_sums(part):
             h_ps = [psum.tile([P, BANK], F32, name=f"h_ps{b}", tag="bank") for b in range(PART_FB // H_IN_BANK)]
             for kb in range(CB):
-                w1_blocks = w1_sb[part][kb // KB_IN_LOAD][:, kb % KB_IN_LOAD, :].rearrange("k (ch p r) -> k ch r p", p=P, r=R)
+                load, row = divmod(kb, KB_IN_LOAD[part])
+                w1_blocks = w1_sb[part][load][:, row, :].rearrange("k (ch p r) -> k ch r p", p=P, r=R)
                 for t in range(PART_FB):
                     b, i = divmod(t, H_IN_BANK)
                     nc.tensor.matmul(
@@ -92,6 +83,11 @@ def tile_block_kernel(tc, base, x, w1, b1, w2, b2, offs, out):
                         start=(kb == 0 and i == 0),
                         stop=(kb == CB - 1 and i == H_IN_BANK - 1),
                     )
+            return h_ps
+
+        h_sb = []
+
+        def gelu_of(part, h_ps):
             for t in range(PART_FB):
                 b, i = divmod(t, H_IN_BANK)
                 ch, r = divmod(part * PART_FB + t, R)
@@ -100,6 +96,21 @@ def tile_block_kernel(tc, base, x, w1, b1, w2, b2, offs, out):
                     h_block[:], h_ps[b][:, i * N : (i + 1) * N], GELU, bias=b1_cols[:, r, ch : ch + 1]
                 )
                 h_sb.append(h_block)
+
+        first_sums = hidden_sums(0)
+
+        identity = held.tile([CHUNKS, CHUNKS], F32, name="identity")
+        make_identity(nc, identity[:])
+        b1_blocks = b1_rows[:].rearrange("ch (p r) -> ch r p", r=R)
+        b1_ps = psum.tile([P, R, CHUNKS], F32, name="b1_ps", tag="bank")
+        for r in range(R):
+            nc.tensor.matmul(b1_ps[:, r, :], b1_blocks[:, r, :], identity[:], start=True, stop=True)
+        b1_cols = held.tile([P, R, CHUNKS], F32, name="b1_cols")
+        nc.vector.tensor_copy(b1_cols[:], b1_ps[:])
+
+        gelu_of(0, first_sums)
+        for part in range(1, PARTS):
+            gelu_of(part, hidden_sums(part))
 
         ff_ps = [psum.tile([P, N], F32, name=f"ff_ps{cb}", tag="bank") for cb in range(CB)]
         for ch in range(CHUNKS):

@@ -4,9 +4,12 @@ from concourse.masks import make_identity
 P = 128
 C, F, S, N = 768, 3072, 256, 128
 CB = C // P
+GROUPS = 3
+J = CB // GROUPS
 FB = F // P
 R = 4
 CHUNKS = FB // R
+LATE = 3
 PARTS = 2
 PART_FB = FB // PARTS
 KB_IN_LOAD = (1, 2)
@@ -30,41 +33,55 @@ def tile_block_kernel(tc, base, x, w1, b1, w2, b2, offs, out):
     ):
 
         x_bf = held.tile([P, CB, N], BF16, name="x_bf")
-        nc.sync.dma_start(x_bf[:], x.rearrange("(p kb) j -> p kb j", kb=CB))
+        nc.sync.dma_start(
+            x_bf[:].rearrange("p (g j) n -> p g j n", j=J), x.rearrange("(g p j) n -> p g j n", p=P, j=J)
+        )
 
         b1_rows = held.tile([CHUNKS, R * P], F32, name="b1_rows")
         nc.scalar.dma_start(b1_rows[:], b1.rearrange("(ch m) o -> ch (m o)", ch=CHUNKS))
 
-        w1_view = w1.rearrange("(p kb) f -> p kb f", kb=CB)
+        w1_view = w1.rearrange("(g p j) f -> p g j f", p=P, j=J)
         w1_sb = []
         for part in range(PARTS):
             w1_part = []
             for kb in range(0, CB, KB_IN_LOAD[part]):
+                g, j = divmod(kb, J)
                 w1_rows = held.tile([P, KB_IN_LOAD[part], PART_FB * P], BF16, name=f"w1_rows{part}_{kb}")
                 nc.sync.dma_start(
-                    w1_rows[:], w1_view[:, kb : kb + KB_IN_LOAD[part], part * PART_FB * P : (part + 1) * PART_FB * P]
+                    w1_rows[:], w1_view[:, g, j : j + KB_IN_LOAD[part], part * PART_FB * P : (part + 1) * PART_FB * P]
                 )
                 w1_part.append(w1_rows)
             w1_sb.append(w1_part)
 
         w2_view = w2.rearrange("(ch p r) c -> ch p r c", p=P, r=R)
-        w2_sb = []
-        for ch in range(CHUNKS):
-            w2_rows = held.tile([P, R, C], BF16, name=f"w2_rows{ch}")
-            nc.sync.dma_start(w2_rows[:], w2_view[ch])
-            w2_sb.append(w2_rows)
+        w2_rows = []
+        for ch in range(CHUNKS - LATE):
+            w2_chunk = held.tile([P, R, C], BF16, name=f"w2_chunk{ch}")
+            nc.sync.dma_start(w2_chunk[:], w2_view[ch])
+            w2_rows.append(w2_chunk)
 
         b2_cols = held.tile([P, CB], F32, name="b2_cols")
-        nc.sync.dma_start(b2_cols[:], b2.rearrange("(p cb) o -> p (cb o)", cb=CB))
+        nc.sync.dma_start(
+            b2_cols[:].rearrange("p (g j) -> p g j", j=J), b2.rearrange("(g p j) o -> p g (j o)", p=P, j=J)
+        )
         offsets = held.tile([P, N // 16], U16, name="offsets")
         nc.sync.dma_start(offsets[:], offs)
-        base_view = base.rearrange("(p cb) s -> cb p s", cb=CB)
-        out_view = out.rearrange("(p cb) s -> cb p s", cb=CB)
+
+        base_view = base.rearrange("(g p j) s -> g j p s", p=P, j=J)
+        out_view = out.rearrange("(g p j) s -> g j p s", p=P, j=J)
+        w2_cols = []
         windows = []
-        for cb in range(CB):
-            window = held.tile([P, S], F32, name=f"window{cb}")
-            nc.sync.dma_start(window[:], base_view[cb])
-            windows.append(window)
+        for g in range(GROUPS):
+            w2_group = []
+            for ch in range(CHUNKS - LATE, CHUNKS):
+                w2_piece = held.tile([P, R, J * P], BF16, name=f"w2_piece{g}_{ch}")
+                nc.sync.dma_start(w2_piece[:], w2_view[ch][:, :, g * J * P : (g + 1) * J * P])
+                w2_group.append(w2_piece)
+            w2_cols.append(w2_group)
+            for j in range(J):
+                window = held.tile([P, S], F32, name=f"window{g}_{j}")
+                nc.sync.dma_start(window[:], base_view[g, j])
+                windows.append(window)
 
         x_f32 = held.tile([P, CB, N], F32, name="x_f32")
         nc.vector.tensor_copy(x_f32[:], x_bf[:])
@@ -113,20 +130,32 @@ def tile_block_kernel(tc, base, x, w1, b1, w2, b2, offs, out):
             gelu_of(part, hidden_sums(part))
 
         ff_ps = [psum.tile([P, N], F32, name=f"ff_ps{cb}", tag="bank") for cb in range(CB)]
-        for ch in range(CHUNKS):
-            w2_blocks = w2_sb[ch][:].rearrange("f r (p cb) -> f r cb p", cb=CB)
-            for cb in range(CB):
-                for r in range(R):
-                    nc.tensor.matmul(
-                        ff_ps[cb][:],
-                        w2_blocks[:, r, cb, :],
-                        h_sb[ch * R + r][:],
-                        start=(ch == 0 and r == 0),
-                        stop=(ch == CHUNKS - 1 and r == R - 1),
-                    )
 
-        for cb in range(CB):
-            ff = work.tile([P, N], F32, name="ff")
-            nc.scalar.activation(ff[:], ff_ps[cb][:], IDENTITY, bias=b2_cols[:, cb : cb + 1])
-            nc.vector.tensor_tensor(windows[cb][:].indirect(offsets[:]), ff[:], x_f32[:, cb, :], ADD)
-            nc.sync.dma_start(out_view[cb], windows[cb][:])
+        def add_chunk(g, j, ch):
+            if ch < CHUNKS - LATE:
+                w2_blocks = w2_rows[ch][:].rearrange("f r (g p j) -> f r g j p", p=P, j=J)[:, :, g, j, :]
+            else:
+                w2_blocks = w2_cols[g][ch - (CHUNKS - LATE)][:].rearrange("f r (p j) -> f r j p", j=J)[:, :, j, :]
+            for r in range(R):
+                nc.tensor.matmul(
+                    ff_ps[g * J + j][:],
+                    w2_blocks[:, r, :],
+                    h_sb[ch * R + r][:],
+                    start=(ch == 0 and r == 0),
+                    stop=(ch == CHUNKS - 1 and r == R - 1),
+                )
+
+        for ch in range(CHUNKS - LATE):
+            for g in range(GROUPS):
+                for j in range(J):
+                    add_chunk(g, j, ch)
+
+        for g in range(GROUPS):
+            for j in range(J):
+                cb = g * J + j
+                for ch in range(CHUNKS - LATE, CHUNKS):
+                    add_chunk(g, j, ch)
+                ff = work.tile([P, N], F32, name="ff")
+                nc.scalar.activation(ff[:], ff_ps[cb][:], IDENTITY, bias=b2_cols[:, cb : cb + 1])
+                nc.vector.tensor_tensor(windows[cb][:].indirect(offsets[:]), ff[:], x_f32[:, cb, :], ADD)
+                nc.sync.dma_start(out_view[g, j], windows[cb][:])

@@ -9,7 +9,7 @@ J = CB // GROUPS
 FB = F // P
 R = 4
 CHUNKS = FB // R
-LATE = 3
+LATE = 2
 PARTS = 2
 PART_FB = FB // PARTS
 KB_IN_LOAD = (1, 2)

@@ -10,8 +10,9 @@ FB = F // P
 R = 4
 CHUNKS = FB // R
 LATE = 2
-PARTS = 2
-PART_FB = FB // PARTS
+PART_FB = ((CHUNKS - LATE) * R, LATE * R)
+PART_AT = (0, (CHUNKS - LATE) * R)
+PARTS = len(PART_FB)
 KB_IN_LOAD = (1, 2)
 BANK = 512
 H_IN_BANK = BANK // N
@@ -46,9 +47,10 @@ def tile_block_kernel(tc, base, x, w1, b1, w2, b2, offs, out):
             w1_part = []
             for kb in range(0, CB, KB_IN_LOAD[part]):
                 g, j = divmod(kb, J)
-                w1_rows = held.tile([P, KB_IN_LOAD[part], PART_FB * P], BF16, name=f"w1_rows{part}_{kb}")
+                w1_rows = held.tile([P, KB_IN_LOAD[part], PART_FB[part] * P], BF16, name=f"w1_rows{part}_{kb}")
                 nc.sync.dma_start(
-                    w1_rows[:], w1_view[:, g, j : j + KB_IN_LOAD[part], part * PART_FB * P : (part + 1) * PART_FB * P]
+                    w1_rows[:],
+                    w1_view[:, g, j : j + KB_IN_LOAD[part], PART_AT[part] * P : (PART_AT[part] + PART_FB[part]) * P],
                 )
                 w1_part.append(w1_rows)
             w1_sb.append(w1_part)
@@ -87,11 +89,11 @@ def tile_block_kernel(tc, base, x, w1, b1, w2, b2, offs, out):
         nc.vector.tensor_copy(x_f32[:], x_bf[:])
 
         def hidden_sums(part):
-            h_ps = [psum.tile([P, BANK], F32, name=f"h_ps{b}", tag="bank") for b in range(PART_FB // H_IN_BANK)]
+            h_ps = [psum.tile([P, BANK], F32, name=f"h_ps{b}", tag="bank") for b in range(PART_FB[part] // H_IN_BANK)]
             for kb in range(CB):
                 load, row = divmod(kb, KB_IN_LOAD[part])
                 w1_blocks = w1_sb[part][load][:, row, :].rearrange("k (ch p r) -> k ch r p", p=P, r=R)
-                for t in range(PART_FB):
+                for t in range(PART_FB[part]):
                     b, i = divmod(t, H_IN_BANK)
                     nc.tensor.matmul(
                         h_ps[b][:, i * N : (i + 1) * N],
@@ -105,9 +107,9 @@ def tile_block_kernel(tc, base, x, w1, b1, w2, b2, offs, out):
         h_sb = []
 
         def gelu_of(part, h_ps):
-            for t in range(PART_FB):
+            for t in range(PART_FB[part]):
                 b, i = divmod(t, H_IN_BANK)
-                ch, r = divmod(part * PART_FB + t, R)
+                ch, r = divmod(PART_AT[part] + t, R)
                 h_block = held.tile([P, N], BF16, name=f"h_block{ch}_{r}")
                 nc.scalar.activation(
                     h_block[:], h_ps[b][:, i * N : (i + 1) * N], GELU, bias=b1_cols[:, r, ch : ch + 1]

import concourse.mybir as mybir
from concourse.masks import make_identity

P = 128
C, F, S, N = 768, 3072, 256, 128
CB = C // P
GROUPS = 3
J = CB // GROUPS
FB = F // P
R = 4
CHUNKS = FB // R
LATE = 2
PART_FB = ((CHUNKS - LATE) * R, LATE * R)
PART_AT = (0, (CHUNKS - LATE) * R)
PARTS = len(PART_FB)
KB_IN_LOAD = (1, 2)
BANK = 512
H_IN_BANK = BANK // N

FLOPS = 2 * 2 * C * F * N

BF16, F32, U16 = mybir.dt.bfloat16, mybir.dt.float32, mybir.dt.uint16
GELU = mybir.ActivationFunctionType.Gelu
IDENTITY = mybir.ActivationFunctionType.Identity
ADD = mybir.AluOpType.add


def tile_block_kernel(tc, base, x, w1, b1, w2, b2, offs, out):
    nc = tc.nc
    with (
        tc.tile_pool(name="held", bufs=1) as held,
        tc.tile_pool(name="work", bufs=3) as work,
        tc.psum_pool(name="psum", bufs=8) as psum,
    ):

        x_bf = held.tile([P, CB, N], BF16, name="x_bf")
        nc.sync.dma_start(
            x_bf[:].rearrange("p (g j) n -> p g j n", j=J), x.rearrange("(g p j) n -> p g j n", p=P, j=J)
        )

        b1_rows = held.tile([CHUNKS, R * P], F32, name="b1_rows")
        nc.scalar.dma_start(b1_rows[:], b1.rearrange("(ch m) o -> ch (m o)", ch=CHUNKS))

        w1_view = w1.rearrange("(g p j) f -> p g j f", p=P, j=J)
        w1_sb = []
        for part in range(PARTS):
            w1_part = []
            for kb in range(0, CB, KB_IN_LOAD[part]):
                g, j = divmod(kb, J)
                w1_rows = held.tile([P, KB_IN_LOAD[part], PART_FB[part] * P], BF16, name=f"w1_rows{part}_{kb}")
                nc.sync.dma_start(
                    w1_rows[:],
                    w1_view[:, g, j : j + KB_IN_LOAD[part], PART_AT[part] * P : (PART_AT[part] + PART_FB[part]) * P],
                )
                w1_part.append(w1_rows)
            w1_sb.append(w1_part)

        w2_view = w2.rearrange("(ch p r) c -> ch p r c", p=P, r=R)
        w2_rows = []
        for ch in range(CHUNKS - LATE):
            w2_chunk = held.tile([P, R, C], BF16, name=f"w2_chunk{ch}")
            nc.sync.dma_start(w2_chunk[:], w2_view[ch])
            w2_rows.append(w2_chunk)

        b2_cols = held.tile([P, CB], F32, name="b2_cols")
        nc.sync.dma_start(
            b2_cols[:].rearrange("p (g j) -> p g j", j=J), b2.rearrange("(g p j) o -> p g (j o)", p=P, j=J)
        )
        offsets = held.tile([P, N // 16], U16, name="offsets")
        nc.sync.dma_start(offsets[:], offs)

        base_view = base.rearrange("(g p j) s -> g j p s", p=P, j=J)
        out_view = out.rearrange("(g p j) s -> g j p s", p=P, j=J)
        w2_cols = []
        windows = []
        for g in range(GROUPS):
            w2_group = []
            for ch in range(CHUNKS - LATE, CHUNKS):
                w2_piece = held.tile([P, R, J * P], BF16, name=f"w2_piece{g}_{ch}")
                nc.sync.dma_start(w2_piece[:], w2_view[ch][:, :, g * J * P : (g + 1) * J * P])
                w2_group.append(w2_piece)
            w2_cols.append(w2_group)
            for j in range(J):
                window = held.tile([P, S], F32, name=f"window{g}_{j}")
                nc.sync.dma_start(window[:], base_view[g, j])
                windows.append(window)

        x_f32 = held.tile([P, CB, N], F32, name="x_f32")
        nc.vector.tensor_copy(x_f32[:], x_bf[:])

        def hidden_sums(part):
            h_ps = [psum.tile([P, BANK], F32, name=f"h_ps{b}", tag="bank") for b in range(PART_FB[part] // H_IN_BANK)]
            for kb in range(CB):
                load, row = divmod(kb, KB_IN_LOAD[part])
                w1_blocks = w1_sb[part][load][:, row, :].rearrange("k (ch p r) -> k ch r p", p=P, r=R)
                for t in range(PART_FB[part]):
                    b, i = divmod(t, H_IN_BANK)
                    nc.tensor.matmul(
                        h_ps[b][:, i * N : (i + 1) * N],
                        w1_blocks[:, t // R, t % R, :],
                        x_bf[:, kb, :],
                        start=(kb == 0 and i == 0),
                        stop=(kb == CB - 1 and i == H_IN_BANK - 1),
                    )
            return h_ps

        h_sb = []

        def gelu_of(part, h_ps):
            for t in range(PART_FB[part]):
                b, i = divmod(t, H_IN_BANK)
                ch, r = divmod(PART_AT[part] + t, R)
                h_block = held.tile([P, N], BF16, name=f"h_block{ch}_{r}")
                nc.scalar.activation(
                    h_block[:], h_ps[b][:, i * N : (i + 1) * N], GELU, bias=b1_cols[:, r, ch : ch + 1]
                )
                h_sb.append(h_block)

        first_sums = hidden_sums(0)

        identity = held.tile([CHUNKS, CHUNKS], F32, name="identity")
        make_identity(nc, identity[:])
        b1_blocks = b1_rows[:].rearrange("ch (p r) -> ch r p", r=R)
        b1_ps = psum.tile([P, R, CHUNKS], F32, name="b1_ps", tag="bank")
        for r in range(R):
            nc.tensor.matmul(b1_ps[:, r, :], b1_blocks[:, r, :], identity[:], start=True, stop=True)
        b1_cols = held.tile([P, R, CHUNKS], F32, name="b1_cols")
        nc.vector.tensor_copy(b1_cols[:], b1_ps[:])

        gelu_of(0, first_sums)
        for part in range(1, PARTS):
            gelu_of(part, hidden_sums(part))

        ff_ps = [psum.tile([P, N], F32, name=f"ff_ps{cb}", tag="bank") for cb in range(CB)]

        def add_chunk(g, j, ch):
            if ch < CHUNKS - LATE:
                w2_blocks = w2_rows[ch][:].rearrange("f r (g p j) -> f r g j p", p=P, j=J)[:, :, g, j, :]
            else:
                w2_blocks = w2_cols[g][ch - (CHUNKS - LATE)][:].rearrange("f r (p j) -> f r j p", j=J)[:, :, j, :]
            for r in range(R):
                nc.tensor.matmul(
                    ff_ps[g * J + j][:],
                    w2_blocks[:, r, :],
                    h_sb[ch * R + r][:],
                    start=(ch == 0 and r == 0),
                    stop=(ch == CHUNKS - 1 and r == R - 1),
                )

        for ch in range(CHUNKS - LATE):
            for g in range(GROUPS):
                for j in range(J):
                    add_chunk(g, j, ch)

        for g in range(GROUPS):
            for j in range(J):
                cb = g * J + j
                for ch in range(CHUNKS - LATE, CHUNKS):
                    add_chunk(g, j, ch)
                ff = work.tile([P, N], F32, name="ff")
                nc.scalar.activation(ff[:], ff_ps[cb][:], IDENTITY, bias=b2_cols[:, cb : cb + 1])
                nc.vector.tensor_tensor(windows[cb][:].indirect(offsets[:]), ff[:], x_f32[:, cb, :], ADD)
                nc.sync.dma_start(out_view[g, j], windows[cb][:])
